import numpy as np
import ml_dtypes


def mxq(x, axis, fmt="e4m3"):
    dtype, down = {"e4m3": (ml_dtypes.float8_e4m3fn, 7), "e5m2": (ml_dtypes.float8_e5m2, 14)}[fmt]
    v = np.moveaxis(np.asarray(x, np.float32).astype(ml_dtypes.bfloat16).astype(np.float64), axis, -1)
    blocks = v.reshape(v.shape[:-1] + (-1, 32))
    amax = np.abs(blocks).max(-1, keepdims=True)
    byte = np.maximum(np.where(amax > 0, np.frexp(amax)[1] - 1 + 127, 0) - down, 1)
    scale = np.exp2(byte - 127.0)
    codes = (blocks / scale).astype(np.float32).astype(dtype).astype(np.float64)
    return np.moveaxis((codes * scale).reshape(v.shape), -1, axis)


WIDE = False


def mx_kscale(k):
    if not WIDE:
        return np.ones(k)
    levels = np.array([10, -10, 5, -5, 0])
    a = np.random.permutation(np.resize(levels, k // 512 * 4)).reshape(k // 512, 4)
    idx = np.arange(k)
    return np.exp2(a[idx // 512, idx % 128 // 32])


BF16 = ml_dtypes.bfloat16


def bf(x):
    return np.asarray(x, np.float32).astype(BF16)


def f64(x):
    return np.asarray(x).astype(np.float64)


M, K, N = 8192, 1024, 512

THRESHOLD = 0.05
EPS = 1e-6


def ternarize_ste(weight):
    scale = np.maximum(np.mean(np.abs(weight)), EPS)
    t = THRESHOLD * scale
    ternary = np.where(weight > t, 1.0, np.where(weight < -t, -1.0, 0.0))
    return weight + (ternary - weight)


def setup_inputs():
    bound = 1.0 / np.sqrt(K)
    s = mx_kscale(K)
    r = s / s.min()
    keep = np.where(r <= 4.0, 1.0, 2.0 ** -20)
    return {"x": bf(np.random.standard_normal((M, K)) * 4.0 / np.sqrt(K) * r[None, :]),
            "weight": bf(np.random.uniform(-bound, bound, (N, K)) * keep[None, :]),
            "bias": bf(np.random.standard_normal(N) * 0.5)}


def reference(x, weight, bias):
    q_weight = ternarize_ste(f64(weight))
    return (mxq(f64(x), 1, "e4m3") @ mxq(q_weight, 1, "e4m3").T) + f64(bias)

@@ -1,0 +1,195 @@
+from contextlib import ExitStack
+
+import concourse.mybir as mybir
+from concourse.masks import make_identity
+
+BF16 = mybir.dt.bfloat16
+F32 = mybir.dt.float32
+U32 = mybir.dt.uint32
+U8 = mybir.dt.uint8
+FP8X4 = mybir.dt.float8_e4m3fn_x4
+ALU = mybir.AluOpType
+ACT = mybir.ActivationFunctionType
+AX = mybir.AxisListType
+
+M, K, N = 8192, 1024, 512
+THRESHOLD = 0.05
+EPS = 1e-6
+FLOPS = 2 * M * K * N
+P = 128
+CHUNKS = 16
+LAG = 2
+
+
+def tile_bitlinear_t_kernel(tc, x, weight, bias, out):
+    nc = tc.nc
+    with ExitStack() as ctx:
+        const = ctx.enter_context(tc.tile_pool(name="const", bufs=1))
+        ring = ctx.enter_context(tc.tile_pool(name="ring", bufs=10))
+        grp = ctx.enter_context(tc.tile_pool(name="grp", bufs=3))
+        cod = ctx.enter_context(tc.tile_pool(name="cod", bufs=3))
+        ps_t = ctx.enter_context(tc.psum_pool(name="ps_t", bufs=4))
+        ps_m = ctx.enter_context(tc.psum_pool(name="ps_m", bufs=4))
+        ctx.enter_context(tc.manual_schedule())
+
+        ident = const.tile([P, P], F32, name="ident")
+        make_identity(nc, ident[:])
+        brow = const.tile([P, N], BF16, name="brow")
+        nc.vector.memset(brow[:], 0.0)
+        nc.scalar.dma_start(out=brow[0:1, :], in_=bias.rearrange("(o n) -> o n", o=1))
+        ones_f = const.tile([P, P], F32, name="ones_f")
+        nc.vector.memset(ones_f[:], 1.0)
+        ones_b = const.tile([P, P], BF16, name="ones_b")
+        nc.vector.memset(ones_b[:], 1.0)
+
+        w_nat = ring.tile([P, 4, K], BF16, tag="big", name="w_nat", align_bytes=64)
+        for nt in range(4):
+            nc.sync.dma_start(out=w_nat[:, nt, :], in_=weight[nt * P:(nt + 1) * P, :])
+        wq = ring.tile([P, 8 * K], BF16, tag="big", name="wq", align_bytes=64)
+        xs = []
+        for s in range(8):
+            xt = ring.tile([P, 8, K], BF16, tag="big", name="xs%d" % s, align_bytes=64)
+            xs.append(xt)
+            if s < 2:
+                for h in range(2):
+                    r0 = 1024 * s + 512 * h
+                    nc.sync.dma_start(
+                        out=xt[:, 4 * h:4 * h + 4, :],
+                        in_=x[r0:r0 + 512, :].rearrange("(p j) k -> p j k", j=4),
+                    )
+            else:
+                nc.sync.dma_start(
+                    out=xt[:],
+                    in_=x[1024 * s:1024 * (s + 1), :].rearrange("(p j) k -> p j k", j=8),
+                )
+
+        junk_s = const.tile([P, K], BF16, name="junk_s")
+        junk_v = const.tile([P, K], BF16, name="junk_v")
+        acc_s = const.tile([P, 2], F32, name="acc_s")
+        acc_v = const.tile([P, 2], F32, name="acc_v")
+        for i in range(2):
+            nc.scalar.activation(
+                out=junk_s[:], in_=w_nat[:, 2 * i, :], func=ACT.Abs, accum_out=acc_s[:, i:i + 1]
+            )
+            nc.vector.scalar_tensor_tensor(
+                out=junk_v[:], in0=w_nat[:, 2 * i + 1, :], scalar=-1.0, in1=w_nat[:, 2 * i + 1, :],
+                op0=ALU.mult, op1=ALU.max, accum_out=acc_v[:, i:i + 1],
+            )
+
+        wg_words = wq[:, 0:4 * K].bitcast(F32).rearrange("p (g n u) -> p g n u", g=2, u=2)
+        for nt in range(4):
+            bank = ps_t.tile([P, 4, P], F32, tag="tp", name="wt%d" % nt)
+            wv = w_nat[:, nt, :].bitcast(F32)
+            for b in range(4):
+                nc.tensor.transpose(bank[:, b, :], wv[:, P * b:P * (b + 1)], ident[:])
+            nc.scalar.copy(
+                out=wg_words[:, :, nt * P:(nt + 1) * P, :],
+                in_=bank[:].rearrange("p (g u) n -> p g n u", u=2),
+            )
+
+        tot = ps_m.tile([P, 2], F32, tag="acc", name="tot")
+        nc.tensor.matmul(tot[:], lhsT=ones_f[:], rhs=acc_s[:], start=True, stop=False)
+        nc.tensor.matmul(tot[:], lhsT=ones_f[:], rhs=acc_v[:], start=False, stop=True)
+        tsum = const.tile([P, 1], F32, name="tsum")
+        nc.vector.tensor_reduce(out=tsum[:], in_=tot[:], axis=AX.X, op=ALU.add)
+        thr = const.tile([P, 2], F32, name="thr")
+        cmean = THRESHOLD / (N * K)
+        nc.vector.tensor_scalar(
+            out=thr[:, 0:1], in0=tsum[:], scalar1=cmean, scalar2=THRESHOLD * EPS,
+            op0=ALU.mult, op1=ALU.max,
+        )
+        nc.vector.tensor_scalar(
+            out=thr[:, 1:2], in0=tsum[:], scalar1=-cmean, scalar2=-THRESHOLD * EPS,
+            op0=ALU.mult, op1=ALU.min,
+        )
+
+        bps = ps_m.tile([P, N], F32, tag="acc", name="bps")
+        nc.tensor.matmul(bps[:], lhsT=ones_b[:], rhs=brow[:], start=True, stop=True)
+        bias_sb = const.tile([P, N], F32, name="bias_sb")
+        nc.scalar.copy(out=bias_sb[:], in_=bps[:])
+
+        qc = const.tile([P, 2, N], U32, name="qc", align_bytes=64)
+        qs = const.tile([P, 2, N], U8, name="qs", align_bytes=64)
+        below = const.tile([P, 4 * N], BF16, name="below")
+
+        def ternarise(g):
+            raw = wq[:, 4 * N * g:4 * N * (g + 1)]
+            q = wq[:, 4 * K + 4 * N * g:4 * K + 4 * N * (g + 1)]
+            nc.vector.tensor_scalar(out=q, in0=raw, scalar1=thr[:, 0:1], scalar2=None, op0=ALU.is_gt)
+            nc.vector.tensor_scalar(out=below[:], in0=raw, scalar1=thr[:, 1:2], scalar2=None, op0=ALU.is_lt)
+            nc.vector.tensor_tensor(out=q, in0=q, in1=below[:], op=ALU.subtract)
+            nc.vector.quantize_mx(out=qc[:, g, :].bitcast(FP8X4), scales=qs[:, g, :], in_=q)
+
+        grouped = {}
+        codes = {}
+        outs = {}
+
+        def transpose_chunk(c):
+            s, h = divmod(c, 2)
+            gt = grp.tile([P, 4 * K], BF16, tag="grp", name="grp%d" % c, align_bytes=64)
+            grouped[c] = gt
+            gw = gt[:].bitcast(F32)
+            for j in range(4):
+                bank = ps_t.tile([P, 4, P], F32, tag="tp", name="xt%d_%d" % (c, j))
+                xv = xs[s][:, 4 * h + j, :].bitcast(F32)
+                for b in range(4):
+                    nc.tensor.transpose(bank[:, b, :], xv[:, P * b:P * (b + 1)], ident[:])
+                nc.scalar.copy(
+                    out=gw[:, 512 * j:512 * (j + 1)].rearrange("p (g r u) -> p g r u", g=2, u=2),
+                    in_=bank[:].rearrange("p (g u) r -> p g r u", u=2),
+                )
+
+        def quantise_chunk(c):
+            cw = cod.tile([P, K], U32, tag="codes", name="cw%d" % c, align_bytes=64)
+            cs = cod.tile([P, K], U8, tag="scl", name="cs%d" % c, align_bytes=64)
+            codes[c] = (cw, cs)
+            nc.vector.quantize_mx(out=cw[:].bitcast(FP8X4), scales=cs[:], in_=grouped[c][:])
+
+        def multiply_chunk(c):
+            s, h = divmod(c, 2)
+            if h == 0:
+                outs[s] = ring.tile([P, 8, N], F32, tag="big", name="o%d" % s, align_bytes=64)
+            ot = outs[s]
+            cw, cs = codes[c]
+            for j in range(4):
+                acc = ps_m.tile([P, N], F32, tag="acc", name="acc%d_%d" % (c, j))
+                for g in range(2):
+                    col = (2 * j + g) * P
+                    nc.tensor.matmul_mx(
+                        out=acc[:],
+                        lhsT=cw[:, col:col + P].bitcast(FP8X4),
+                        lhsT_scale=cs[:, col:col + P],
+                        rhs=qc[:, g, :].bitcast(FP8X4),
+                        rhs_scale=qs[:, g, :],
+                        start=(g == 0),
+                        stop=(g == 1),
+                    )
+                nc.vector.tensor_tensor(out=ot[:, 4 * h + j, :], in0=acc[:], in1=bias_sb[:], op=ALU.add)
+                if c == CHUNKS - 1 and j % 2 == 1:
+                    ov = out[1024 * s:1024 * (s + 1), :].rearrange("(p j) n -> p j n", j=8)
+                    nc.sync.dma_start(out=ov[:, 3 + j:5 + j, :], in_=ot[:, 3 + j:5 + j, :])
+            if s < 2:
+                r0 = 512 * c
+                nc.sync.dma_start(
+                    out=out[r0:r0 + 512, :].rearrange("(p j) n -> p j n", j=4),
+                    in_=ot[:, 4 * h:4 * h + 4, :],
+                )
+            elif s < 7:
+                if h == 1:
+                    nc.sync.dma_start(
+                        out=out[1024 * s:1024 * (s + 1), :].rearrange("(p j) n -> p j n", j=8),
+                        in_=ot[:],
+                    )
+            elif h == 0:
+                ov = out[1024 * s:1024 * (s + 1), :].rearrange("(p j) n -> p j n", j=8)
+                nc.sync.dma_start(out=ov[:, 0:4, :], in_=ot[:, 0:4, :])
+
+        for r in range(CHUNKS + LAG):
+            if r < CHUNKS:
+                transpose_chunk(r)
+            if r < 2:
+                ternarise(r)
+            if 1 <= r <= CHUNKS:
+                quantise_chunk(r - 1)
+            if r >= LAG:
+                multiply_chunk(r - LAG)

@@ -18,7 +18,8 @@ EPS = 1e-6
 FLOPS = 2 * M * K * N
 P = 128
 CHUNKS = 16
-LAG = 2
+LAG = 3
+OFFLOAD = False
 
 
 def tile_bitlinear_t_kernel(tc, x, weight, bias, out):
@@ -26,7 +27,7 @@ def tile_bitlinear_t_kernel(tc, x, weight, bias, out):
     with ExitStack() as ctx:
         const = ctx.enter_context(tc.tile_pool(name="const", bufs=1))
         ring = ctx.enter_context(tc.tile_pool(name="ring", bufs=10))
-        grp = ctx.enter_context(tc.tile_pool(name="grp", bufs=3))
+        grp = ctx.enter_context(tc.tile_pool(name="grp", bufs=4))
         cod = ctx.enter_context(tc.tile_pool(name="cod", bufs=3))
         ps_t = ctx.enter_context(tc.psum_pool(name="ps_t", bufs=4))
         ps_m = ctx.enter_context(tc.psum_pool(name="ps_m", bufs=4))
@@ -123,21 +124,29 @@ def tile_bitlinear_t_kernel(tc, x, weight, bias, out):
         grouped = {}
         codes = {}
         outs = {}
+        accs = {}
+
+        def copy_bank(c, j, bank):
+            gw = grouped[c][:].bitcast(F32)
+            nc.scalar.copy(
+                out=gw[:, 512 * j:512 * (j + 1)].rearrange("p (g r u) -> p g r u", g=2, u=2),
+                in_=bank[:].rearrange("p (g u) r -> p g r u", u=2),
+            )
 
         def transpose_chunk(c):
             s, h = divmod(c, 2)
-            gt = grp.tile([P, 4 * K], BF16, tag="grp", name="grp%d" % c, align_bytes=64)
-            grouped[c] = gt
-            gw = gt[:].bitcast(F32)
+            grouped[c] = grp.tile([P, 4 * K], BF16, tag="grp", name="grp%d" % c, align_bytes=64)
+            last = None
             for j in range(4):
                 bank = ps_t.tile([P, 4, P], F32, tag="tp", name="xt%d_%d" % (c, j))
                 xv = xs[s][:, 4 * h + j, :].bitcast(F32)
                 for b in range(4):
                     nc.tensor.transpose(bank[:, b, :], xv[:, P * b:P * (b + 1)], ident[:])
-                nc.scalar.copy(
-                    out=gw[:, 512 * j:512 * (j + 1)].rearrange("p (g r u) -> p g r u", g=2, u=2),
-                    in_=bank[:].rearrange("p (g u) r -> p g r u", u=2),
-                )
+                if j < 3:
+                    copy_bank(c, j, bank)
+                else:
+                    last = bank
+            return last
 
         def quantise_chunk(c):
             cw = cod.tile([P, K], U32, tag="codes", name="cw%d" % c, align_bytes=64)
@@ -145,51 +154,79 @@ def tile_bitlinear_t_kernel(tc, x, weight, bias, out):
             codes[c] = (cw, cs)
             nc.vector.quantize_mx(out=cw[:].bitcast(FP8X4), scales=cs[:], in_=grouped[c][:])
 
-        def multiply_chunk(c):
+        def mx_pass(c, j, g):
+            cw, cs = codes[c]
+            if g == 0:
+                accs[(c, j)] = ps_m.tile([P, N], F32, tag="acc", name="acc%d_%d" % (c, j))
+            col = (2 * j + g) * P
+            nc.tensor.matmul_mx(
+                out=accs[(c, j)][:],
+                lhsT=cw[:, col:col + P].bitcast(FP8X4),
+                lhsT_scale=cs[:, col:col + P],
+                rhs=qc[:, g, :].bitcast(FP8X4),
+                rhs_scale=qs[:, g, :],
+                start=(g == 0),
+                stop=(g == 1),
+            )
+
+        def finish_tile(c, j):
+            s, h = divmod(c, 2)
+            ot = outs[s]
+            dst = ot[:, 4 * h + j, :]
+            if OFFLOAD and j == 0:
+                nc.scalar.copy(out=dst, in_=accs[(c, j)][:])
+                nc.gpsimd.tensor_tensor(out=dst, in0=dst, in1=bias_sb[:], op=ALU.add)
+            else:
+                nc.vector.tensor_tensor(out=dst, in0=accs[(c, j)][:], in1=bias_sb[:], op=ALU.add)
+
+        def store_after(c, j):
+            s, h = divmod(c, 2)
+            ot = outs[s]
+            if s < 2:
+                if j == 3:
+                    r0 = 512 * c
+                    nc.sync.dma_start(
+                        out=out[r0:r0 + 512, :].rearrange("(p j) n -> p j n", j=4),
+                        in_=ot[:, 4 * h:4 * h + 4, :],
+                    )
+                return
+            ov = out[1024 * s:1024 * (s + 1), :].rearrange("(p j) n -> p j n", j=8)
+            if s < 7:
+                if h == 1 and j == 3:
+                    nc.sync.dma_start(out=ov, in_=ot[:])
+            elif h == 0:
+                if j == 3:
+                    nc.sync.dma_start(out=ov[:, 0:4, :], in_=ot[:, 0:4, :])
+            elif j % 2 == 1:
+                nc.sync.dma_start(out=ov[:, 3 + j:5 + j, :], in_=ot[:, 3 + j:5 + j, :])
+
+        def multiply_chunk(c, last_bank, first_pass_done):
             s, h = divmod(c, 2)
             if h == 0:
                 outs[s] = ring.tile([P, 8, N], F32, tag="big", name="o%d" % s, align_bytes=64)
-            ot = outs[s]
-            cw, cs = codes[c]
             for j in range(4):
-                acc = ps_m.tile([P, N], F32, tag="acc", name="acc%d_%d" % (c, j))
-                for g in range(2):
-                    col = (2 * j + g) * P
-                    nc.tensor.matmul_mx(
-                        out=acc[:],
-                        lhsT=cw[:, col:col + P].bitcast(FP8X4),
-                        lhsT_scale=cs[:, col:col + P],
-                        rhs=qc[:, g, :].bitcast(FP8X4),
-                        rhs_scale=qs[:, g, :],
-                        start=(g == 0),
-                        stop=(g == 1),
-                    )
-                nc.vector.tensor_tensor(out=ot[:, 4 * h + j, :], in0=acc[:], in1=bias_sb[:], op=ALU.add)
-                if c == CHUNKS - 1 and j % 2 == 1:
-                    ov = out[1024 * s:1024 * (s + 1), :].rearrange("(p j) n -> p j n", j=8)
-                    nc.sync.dma_start(out=ov[:, 3 + j:5 + j, :], in_=ot[:, 3 + j:5 + j, :])
-            if s < 2:
-                r0 = 512 * c
-                nc.sync.dma_start(
-                    out=out[r0:r0 + 512, :].rearrange("(p j) n -> p j n", j=4),
-                    in_=ot[:, 4 * h:4 * h + 4, :],
-                )
-            elif s < 7:
-                if h == 1:
-                    nc.sync.dma_start(
-                        out=out[1024 * s:1024 * (s + 1), :].rearrange("(p j) n -> p j n", j=8),
-                        in_=ot[:],
-                    )
-            elif h == 0:
-                ov = out[1024 * s:1024 * (s + 1), :].rearrange("(p j) n -> p j n", j=8)
-                nc.sync.dma_start(out=ov[:, 0:4, :], in_=ot[:, 0:4, :])
+                if not first_pass_done:
+                    mx_pass(c, j, 0)
+                mx_pass(c, j, 1)
+                finish_tile(c, j)
+                if j == 0 and last_bank is not None:
+                    copy_bank(c + LAG, 3, last_bank)
+                store_after(c, j)
 
         for r in range(CHUNKS + LAG):
+            last = None
             if r < CHUNKS:
-                transpose_chunk(r)
-            if r < 2:
-                ternarise(r)
-            if 1 <= r <= CHUNKS:
-                quantise_chunk(r - 1)
+                last = transpose_chunk(r)
+            if r < LAG and last is not None:
+                copy_bank(r, 3, last)
+                last = None
+            if r == 0:
+                ternarise(0)
+            if 2 <= r < CHUNKS + 2:
+                quantise_chunk(r - 2)
+            if r == 2:
+                for j in range(4):
+                    mx_pass(0, j, 0)
+                ternarise(1)
             if r >= LAG:
-                multiply_chunk(r - LAG)
+                multiply_chunk(r - LAG, last, r == LAG)

@@ -19,7 +19,7 @@ FLOPS = 2 * M * K * N
 P = 128
 CHUNKS = 16
 LAG = 3
-OFFLOAD = False
+OFFLOAD = True
 
 
 def tile_bitlinear_t_kernel(tc, x, weight, bias, out):

@@ -51,18 +51,12 @@ def tile_bitlinear_t_kernel(tc, x, weight, bias, out):
         for s in range(8):
             xt = ring.tile([P, 8, K], BF16, tag="big", name="xs%d" % s, align_bytes=64)
             xs.append(xt)
+            xv8 = x[1024 * s:1024 * (s + 1), :].rearrange("(p j) k -> p j k", j=8)
             if s < 2:
                 for h in range(2):
-                    r0 = 1024 * s + 512 * h
-                    nc.sync.dma_start(
-                        out=xt[:, 4 * h:4 * h + 4, :],
-                        in_=x[r0:r0 + 512, :].rearrange("(p j) k -> p j k", j=4),
-                    )
+                    nc.sync.dma_start(out=xt[:, 4 * h:4 * h + 4, :], in_=xv8[:, 4 * h:4 * h + 4, :])
             else:
-                nc.sync.dma_start(
-                    out=xt[:],
-                    in_=x[1024 * s:1024 * (s + 1), :].rearrange("(p j) k -> p j k", j=8),
-                )
+                nc.sync.dma_start(out=xt[:], in_=xv8)
 
         junk_s = const.tile([P, K], BF16, name="junk_s")
         junk_v = const.tile([P, K], BF16, name="junk_v")
@@ -182,21 +176,13 @@ def tile_bitlinear_t_kernel(tc, x, weight, bias, out):
         def store_after(c, j):
             s, h = divmod(c, 2)
             ot = outs[s]
-            if s < 2:
-                if j == 3:
-                    r0 = 512 * c
-                    nc.sync.dma_start(
-                        out=out[r0:r0 + 512, :].rearrange("(p j) n -> p j n", j=4),
-                        in_=ot[:, 4 * h:4 * h + 4, :],
-                    )
-                return
             ov = out[1024 * s:1024 * (s + 1), :].rearrange("(p j) n -> p j n", j=8)
-            if s < 7:
+            if s < 6:
                 if h == 1 and j == 3:
                     nc.sync.dma_start(out=ov, in_=ot[:])
-            elif h == 0:
+            elif c < CHUNKS - 1:
                 if j == 3:
-                    nc.sync.dma_start(out=ov[:, 0:4, :], in_=ot[:, 0:4, :])
+                    nc.sync.dma_start(out=ov[:, 4 * h:4 * h + 4, :], in_=ot[:, 4 * h:4 * h + 4, :])
             elif j % 2 == 1:
                 nc.sync.dma_start(out=ov[:, 3 + j:5 + j, :], in_=ot[:, 3 + j:5 + j, :])
 

@@ -19,7 +19,6 @@ FLOPS = 2 * M * K * N
 P = 128
 CHUNKS = 16
 LAG = 3
-OFFLOAD = True
 
 
 def tile_bitlinear_t_kernel(tc, x, weight, bias, out):
@@ -167,7 +166,7 @@ def tile_bitlinear_t_kernel(tc, x, weight, bias, out):
             s, h = divmod(c, 2)
             ot = outs[s]
             dst = ot[:, 4 * h + j, :]
-            if OFFLOAD and j == 0:
+            if c >= CHUNKS - LAG and j == 0:
                 nc.scalar.copy(out=dst, in_=accs[(c, j)][:])
                 nc.gpsimd.tensor_tensor(out=dst, in0=dst, in1=bias_sb[:], op=ALU.add)
             else:

@@ -61,25 +61,28 @@ def tile_bitlinear_t_kernel(tc, x, weight, bias, out):
         junk_v = const.tile([P, K], BF16, name="junk_v")
         acc_s = const.tile([P, 2], F32, name="acc_s")
         acc_v = const.tile([P, 2], F32, name="acc_v")
-        for i in range(2):
-            nc.scalar.activation(
-                out=junk_s[:], in_=w_nat[:, 2 * i, :], func=ACT.Abs, accum_out=acc_s[:, i:i + 1]
-            )
-            nc.vector.scalar_tensor_tensor(
-                out=junk_v[:], in0=w_nat[:, 2 * i + 1, :], scalar=-1.0, in1=w_nat[:, 2 * i + 1, :],
-                op0=ALU.mult, op1=ALU.max, accum_out=acc_v[:, i:i + 1],
-            )
-
         wg_words = wq[:, 0:4 * K].bitcast(F32).rearrange("p (g n u) -> p g n u", g=2, u=2)
         for nt in range(4):
+            i = nt // 2
+            if nt % 2 == 0:
+                nc.scalar.activation(
+                    out=junk_s[:], in_=w_nat[:, nt, :], func=ACT.Abs, accum_out=acc_s[:, i:i + 1]
+                )
+            else:
+                nc.vector.scalar_tensor_tensor(
+                    out=junk_v[:], in0=w_nat[:, nt, :], scalar=-1.0, in1=w_nat[:, nt, :],
+                    op0=ALU.mult, op1=ALU.max, accum_out=acc_v[:, i:i + 1],
+                )
             bank = ps_t.tile([P, 4, P], F32, tag="tp", name="wt%d" % nt)
             wv = w_nat[:, nt, :].bitcast(F32)
             for b in range(4):
                 nc.tensor.transpose(bank[:, b, :], wv[:, P * b:P * (b + 1)], ident[:])
-            nc.scalar.copy(
-                out=wg_words[:, :, nt * P:(nt + 1) * P, :],
-                in_=bank[:].rearrange("p (g u) n -> p g n u", u=2),
-            )
+            dst = wg_words[:, :, nt * P:(nt + 1) * P, :]
+            moved = bank[:].rearrange("p (g u) n -> p g n u", u=2)
+            if nt % 2 == 0:
+                nc.scalar.copy(out=dst, in_=moved)
+            else:
+                nc.vector.tensor_copy(out=dst, in_=moved)
 
         tot = ps_m.tile([P, 2], F32, tag="acc", name="tot")
         nc.tensor.matmul(tot[:], lhsT=ones_f[:], rhs=acc_s[:], start=True, stop=False)

@@ -36,7 +36,6 @@ def tile_bitlinear_t_kernel(tc, x, weight, bias, out):
         make_identity(nc, ident[:])
         brow = const.tile([P, N], BF16, name="brow")
         nc.vector.memset(brow[:], 0.0)
-        nc.scalar.dma_start(out=brow[0:1, :], in_=bias.rearrange("(o n) -> o n", o=1))
         ones_f = const.tile([P, P], F32, name="ones_f")
         nc.vector.memset(ones_f[:], 1.0)
         ones_b = const.tile([P, P], BF16, name="ones_b")
@@ -45,6 +44,7 @@ def tile_bitlinear_t_kernel(tc, x, weight, bias, out):
         w_nat = ring.tile([P, 4, K], BF16, tag="big", name="w_nat", align_bytes=64)
         for nt in range(4):
             nc.sync.dma_start(out=w_nat[:, nt, :], in_=weight[nt * P:(nt + 1) * P, :])
+        nc.sync.dma_start(out=brow[0:1, :], in_=bias.rearrange("(o n) -> o n", o=1))
         wq = ring.tile([P, 8 * K], BF16, tag="big", name="wq", align_bytes=64)
         xs = []
         for s in range(8):

@@ -51,7 +51,7 @@ def tile_bitlinear_t_kernel(tc, x, weight, bias, out):
             xt = ring.tile([P, 8, K], BF16, tag="big", name="xs%d" % s, align_bytes=64)
             xs.append(xt)
             xv8 = x[1024 * s:1024 * (s + 1), :].rearrange("(p j) k -> p j k", j=8)
-            if s < 2:
+            if s < 3:
                 for h in range(2):
                     nc.sync.dma_start(out=xt[:, 4 * h:4 * h + 4, :], in_=xv8[:, 4 * h:4 * h + 4, :])
             else:

@@ -19,15 +19,21 @@ FLOPS = 2 * M * K * N
 P = 128
 CHUNKS = 16
 LAG = 3
+LOADS = (
+    ((0, 1), (1, 2), (2, 3), (3, 4)),
+    ((0, 1), (1, 2), (2, 4)),
+    ((0, 4),),
+    ((0, 4),),
+)
+STORES = ((0, 0, 0, 4), (0, 0, 0, 4), (0, 2, 1, 1), (1,))
 
 
 def tile_bitlinear_t_kernel(tc, x, weight, bias, out):
     nc = tc.nc
     with ExitStack() as ctx:
         const = ctx.enter_context(tc.tile_pool(name="const", bufs=1))
-        ring = ctx.enter_context(tc.tile_pool(name="ring", bufs=10))
-        grp = ctx.enter_context(tc.tile_pool(name="grp", bufs=4))
-        cod = ctx.enter_context(tc.tile_pool(name="cod", bufs=3))
+        ring = ctx.enter_context(tc.tile_pool(name="ring", bufs=5))
+        cod = ctx.enter_context(tc.tile_pool(name="cod", bufs=4))
         ps_t = ctx.enter_context(tc.psum_pool(name="ps_t", bufs=4))
         ps_m = ctx.enter_context(tc.psum_pool(name="ps_m", bufs=4))
         ctx.enter_context(tc.manual_schedule())
@@ -41,21 +47,19 @@ def tile_bitlinear_t_kernel(tc, x, weight, bias, out):
         ones_b = const.tile([P, P], BF16, name="ones_b")
         nc.vector.memset(ones_b[:], 1.0)
 
-        w_nat = ring.tile([P, 4, K], BF16, tag="big", name="w_nat", align_bytes=64)
-        for nt in range(4):
-            nc.sync.dma_start(out=w_nat[:, nt, :], in_=weight[nt * P:(nt + 1) * P, :])
+        w_nat = const.tile([P, 4, K], BF16, name="w_nat", align_bytes=64)
+        w_view = weight.rearrange("(t p) k -> p t k", p=P)
+        for i in range(2):
+            nc.sync.dma_start(out=w_nat[:, 2 * i:2 * i + 2, :], in_=w_view[:, 2 * i:2 * i + 2, :])
         nc.sync.dma_start(out=brow[0:1, :], in_=bias.rearrange("(o n) -> o n", o=1))
-        wq = ring.tile([P, 8 * K], BF16, tag="big", name="wq", align_bytes=64)
+        wq = const.tile([P, 8 * K], BF16, name="wq", align_bytes=64)
         xs = []
-        for s in range(8):
-            xt = ring.tile([P, 8, K], BF16, tag="big", name="xs%d" % s, align_bytes=64)
+        for s in range(4):
+            xt = ring.tile([P, 16, K], BF16, tag="big", name="xs%d" % s, align_bytes=64)
             xs.append(xt)
-            xv8 = x[1024 * s:1024 * (s + 1), :].rearrange("(p j) k -> p j k", j=8)
-            if s < 3:
-                for h in range(2):
-                    nc.sync.dma_start(out=xt[:, 4 * h:4 * h + 4, :], in_=xv8[:, 4 * h:4 * h + 4, :])
-            else:
-                nc.sync.dma_start(out=xt[:], in_=xv8)
+            xv = x[2048 * s:2048 * (s + 1), :].rearrange("(p j) k -> p j k", j=16)
+            for first, last in LOADS[s]:
+                nc.sync.dma_start(out=xt[:, 4 * first:4 * last, :], in_=xv[:, 4 * first:4 * last, :])
 
         junk_s = const.tile([P, K], BF16, name="junk_s")
         junk_v = const.tile([P, K], BF16, name="junk_v")
@@ -117,25 +121,26 @@ def tile_bitlinear_t_kernel(tc, x, weight, bias, out):
             nc.vector.tensor_tensor(out=q, in0=q, in1=below[:], op=ALU.subtract)
             nc.vector.quantize_mx(out=qc[:, g, :].bitcast(FP8X4), scales=qs[:, g, :], in_=q)
 
-        grouped = {}
         codes = {}
         outs = {}
         accs = {}
 
+        def chunk_rows(c):
+            s, h = divmod(c, 4)
+            return xs[s][:, 4 * h:4 * h + 4, :]
+
         def copy_bank(c, j, bank):
-            gw = grouped[c][:].bitcast(F32)
+            words = chunk_rows(c)[:, j, :].bitcast(F32)
             nc.scalar.copy(
-                out=gw[:, 512 * j:512 * (j + 1)].rearrange("p (g r u) -> p g r u", g=2, u=2),
+                out=words.rearrange("p (g r u) -> p g r u", g=2, u=2),
                 in_=bank[:].rearrange("p (g u) r -> p g r u", u=2),
             )
 
         def transpose_chunk(c):
-            s, h = divmod(c, 2)
-            grouped[c] = grp.tile([P, 4 * K], BF16, tag="grp", name="grp%d" % c, align_bytes=64)
             last = None
             for j in range(4):
                 bank = ps_t.tile([P, 4, P], F32, tag="tp", name="xt%d_%d" % (c, j))
-                xv = xs[s][:, 4 * h + j, :].bitcast(F32)
+                xv = chunk_rows(c)[:, j, :].bitcast(F32)
                 for b in range(4):
                     nc.tensor.transpose(bank[:, b, :], xv[:, P * b:P * (b + 1)], ident[:])
                 if j < 3:
@@ -148,7 +153,10 @@ def tile_bitlinear_t_kernel(tc, x, weight, bias, out):
             cw = cod.tile([P, K], U32, tag="codes", name="cw%d" % c, align_bytes=64)
             cs = cod.tile([P, K], U8, tag="scl", name="cs%d" % c, align_bytes=64)
             codes[c] = (cw, cs)
-            nc.vector.quantize_mx(out=cw[:].bitcast(FP8X4), scales=cs[:], in_=grouped[c][:])
+            nc.vector.quantize_mx(
+                out=cw[:].bitcast(FP8X4), scales=cs[:],
+                in_=chunk_rows(c).rearrange("p j k -> p (j k)"),
+            )
 
         def mx_pass(c, j, g):
             cw, cs = codes[c]
@@ -166,32 +174,27 @@ def tile_bitlinear_t_kernel(tc, x, weight, bias, out):
             )
 
         def finish_tile(c, j):
-            s, h = divmod(c, 2)
-            ot = outs[s]
-            dst = ot[:, 4 * h + j, :]
-            if c >= CHUNKS - LAG and j == 0:
-                nc.scalar.copy(out=dst, in_=accs[(c, j)][:])
-                nc.gpsimd.tensor_tensor(out=dst, in0=dst, in1=bias_sb[:], op=ALU.add)
-            else:
-                nc.vector.tensor_tensor(out=dst, in0=accs[(c, j)][:], in1=bias_sb[:], op=ALU.add)
+            s, h = divmod(c, 4)
+            dst = outs[s][:, 4 * h + j, :]
+            nc.vector.tensor_tensor(out=dst, in0=accs[(c, j)][:], in1=bias_sb[:], op=ALU.add)
 
         def store_after(c, j):
-            s, h = divmod(c, 2)
-            ot = outs[s]
-            ov = out[1024 * s:1024 * (s + 1), :].rearrange("(p j) n -> p j n", j=8)
-            if s < 6:
-                if h == 1 and j == 3:
-                    nc.sync.dma_start(out=ov, in_=ot[:])
-            elif c < CHUNKS - 1:
-                if j == 3:
-                    nc.sync.dma_start(out=ov[:, 4 * h:4 * h + 4, :], in_=ot[:, 4 * h:4 * h + 4, :])
-            elif j % 2 == 1:
-                nc.sync.dma_start(out=ov[:, 3 + j:5 + j, :], in_=ot[:, 3 + j:5 + j, :])
+            s, h = divmod(c, 4)
+            ov = out[2048 * s:2048 * (s + 1), :].rearrange("(p j) n -> p j n", j=16)
+            if c >= CHUNKS - LAG:
+                first, last = 4 * h + j - 1, 4 * h + j + 1
+                due = j % 2 == 1
+            else:
+                span = STORES[s][h]
+                first, last = 4 * (h + 1 - span), 4 * (h + 1)
+                due = j == 3 and span > 0
+            if due:
+                nc.sync.dma_start(out=ov[:, first:last, :], in_=outs[s][:, first:last, :])
 
         def multiply_chunk(c, last_bank, first_pass_done):
-            s, h = divmod(c, 2)
+            s, h = divmod(c, 4)
             if h == 0:
-                outs[s] = ring.tile([P, 8, N], F32, tag="big", name="o%d" % s, align_bytes=64)
+                outs[s] = ring.tile([P, 16, N], F32, tag="big", name="o%d" % s, align_bytes=64)
             for j in range(4):
                 if not first_pass_done:
                     mx_pass(c, j, 0)
@@ -210,11 +213,12 @@ def tile_bitlinear_t_kernel(tc, x, weight, bias, out):
                 last = None
             if r == 0:
                 ternarise(0)
-            if 2 <= r < CHUNKS + 2:
-                quantise_chunk(r - 2)
+            if 1 <= r < CHUNKS + 1:
+                quantise_chunk(r - 1)
+            if r == 1:
+                ternarise(1)
             if r == 2:
                 for j in range(4):
                     mx_pass(0, j, 0)
-                ternarise(1)
             if r >= LAG:
                 multiply_chunk(r - LAG, last, r == LAG)

@@ -176,7 +176,11 @@ def tile_bitlinear_t_kernel(tc, x, weight, bias, out):
         def finish_tile(c, j):
             s, h = divmod(c, 4)
             dst = outs[s][:, 4 * h + j, :]
-            nc.vector.tensor_tensor(out=dst, in0=accs[(c, j)][:], in1=bias_sb[:], op=ALU.add)
+            if j == 0 and c < CHUNKS - LAG:
+                nc.scalar.copy(out=dst, in_=accs[(c, j)][:])
+                nc.gpsimd.tensor_tensor(out=dst, in0=dst, in1=bias_sb[:], op=ALU.add)
+            else:
+                nc.vector.tensor_tensor(out=dst, in0=accs[(c, j)][:], in1=bias_sb[:], op=ALU.add)
 
         def store_after(c, j):
             s, h = divmod(c, 4)

from contextlib import ExitStack

import concourse.mybir as mybir
from concourse.masks import make_identity

BF16 = mybir.dt.bfloat16
F32 = mybir.dt.float32
U32 = mybir.dt.uint32
U8 = mybir.dt.uint8
FP8X4 = mybir.dt.float8_e4m3fn_x4
ALU = mybir.AluOpType
ACT = mybir.ActivationFunctionType
AX = mybir.AxisListType

M, K, N = 8192, 1024, 512
THRESHOLD = 0.05
EPS = 1e-6
FLOPS = 2 * M * K * N
P = 128
CHUNKS = 16
LAG = 3
LOADS = (
    ((0, 1), (1, 2), (2, 3), (3, 4)),
    ((0, 1), (1, 2), (2, 4)),
    ((0, 4),),
    ((0, 4),),
)
STORES = ((0, 0, 0, 4), (0, 0, 0, 4), (0, 2, 1, 1), (1,))


def tile_bitlinear_t_kernel(tc, x, weight, bias, out):
    nc = tc.nc
    with ExitStack() as ctx:
        const = ctx.enter_context(tc.tile_pool(name="const", bufs=1))
        ring = ctx.enter_context(tc.tile_pool(name="ring", bufs=5))
        cod = ctx.enter_context(tc.tile_pool(name="cod", bufs=4))
        ps_t = ctx.enter_context(tc.psum_pool(name="ps_t", bufs=4))
        ps_m = ctx.enter_context(tc.psum_pool(name="ps_m", bufs=4))
        ctx.enter_context(tc.manual_schedule())

        ident = const.tile([P, P], F32, name="ident")
        make_identity(nc, ident[:])
        brow = const.tile([P, N], BF16, name="brow")
        nc.vector.memset(brow[:], 0.0)
        ones_f = const.tile([P, P], F32, name="ones_f")
        nc.vector.memset(ones_f[:], 1.0)
        ones_b = const.tile([P, P], BF16, name="ones_b")
        nc.vector.memset(ones_b[:], 1.0)

        w_nat = const.tile([P, 4, K], BF16, name="w_nat", align_bytes=64)
        w_view = weight.rearrange("(t p) k -> p t k", p=P)
        for i in range(2):
            nc.sync.dma_start(out=w_nat[:, 2 * i:2 * i + 2, :], in_=w_view[:, 2 * i:2 * i + 2, :])
        nc.sync.dma_start(out=brow[0:1, :], in_=bias.rearrange("(o n) -> o n", o=1))
        wq = const.tile([P, 8 * K], BF16, name="wq", align_bytes=64)
        xs = []
        for s in range(4):
            xt = ring.tile([P, 16, K], BF16, tag="big", name="xs%d" % s, align_bytes=64)
            xs.append(xt)
            xv = x[2048 * s:2048 * (s + 1), :].rearrange("(p j) k -> p j k", j=16)
            for first, last in LOADS[s]:
                nc.sync.dma_start(out=xt[:, 4 * first:4 * last, :], in_=xv[:, 4 * first:4 * last, :])

        junk_s = const.tile([P, K], BF16, name="junk_s")
        junk_v = const.tile([P, K], BF16, name="junk_v")
        acc_s = const.tile([P, 2], F32, name="acc_s")
        acc_v = const.tile([P, 2], F32, name="acc_v")
        wg_words = wq[:, 0:4 * K].bitcast(F32).rearrange("p (g n u) -> p g n u", g=2, u=2)
        for nt in range(4):
            i = nt // 2
            if nt % 2 == 0:
                nc.scalar.activation(
                    out=junk_s[:], in_=w_nat[:, nt, :], func=ACT.Abs, accum_out=acc_s[:, i:i + 1]
                )
            else:
                nc.vector.scalar_tensor_tensor(
                    out=junk_v[:], in0=w_nat[:, nt, :], scalar=-1.0, in1=w_nat[:, nt, :],
                    op0=ALU.mult, op1=ALU.max, accum_out=acc_v[:, i:i + 1],
                )
            bank = ps_t.tile([P, 4, P], F32, tag="tp", name="wt%d" % nt)
            wv = w_nat[:, nt, :].bitcast(F32)
            for b in range(4):
                nc.tensor.transpose(bank[:, b, :], wv[:, P * b:P * (b + 1)], ident[:])
            dst = wg_words[:, :, nt * P:(nt + 1) * P, :]
            moved = bank[:].rearrange("p (g u) n -> p g n u", u=2)
            if nt % 2 == 0:
                nc.scalar.copy(out=dst, in_=moved)
            else:
                nc.vector.tensor_copy(out=dst, in_=moved)

        tot = ps_m.tile([P, 2], F32, tag="acc", name="tot")
        nc.tensor.matmul(tot[:], lhsT=ones_f[:], rhs=acc_s[:], start=True, stop=False)
        nc.tensor.matmul(tot[:], lhsT=ones_f[:], rhs=acc_v[:], start=False, stop=True)
        tsum = const.tile([P, 1], F32, name="tsum")
        nc.vector.tensor_reduce(out=tsum[:], in_=tot[:], axis=AX.X, op=ALU.add)
        thr = const.tile([P, 2], F32, name="thr")
        cmean = THRESHOLD / (N * K)
        nc.vector.tensor_scalar(
            out=thr[:, 0:1], in0=tsum[:], scalar1=cmean, scalar2=THRESHOLD * EPS,
            op0=ALU.mult, op1=ALU.max,
        )
        nc.vector.tensor_scalar(
            out=thr[:, 1:2], in0=tsum[:], scalar1=-cmean, scalar2=-THRESHOLD * EPS,
            op0=ALU.mult, op1=ALU.min,
        )

        bps = ps_m.tile([P, N], F32, tag="acc", name="bps")
        nc.tensor.matmul(bps[:], lhsT=ones_b[:], rhs=brow[:], start=True, stop=True)
        bias_sb = const.tile([P, N], F32, name="bias_sb")
        nc.scalar.copy(out=bias_sb[:], in_=bps[:])

        qc = const.tile([P, 2, N], U32, name="qc", align_bytes=64)
        qs = const.tile([P, 2, N], U8, name="qs", align_bytes=64)
        below = const.tile([P, 4 * N], BF16, name="below")

        def ternarise(g):
            raw = wq[:, 4 * N * g:4 * N * (g + 1)]
            q = wq[:, 4 * K + 4 * N * g:4 * K + 4 * N * (g + 1)]
            nc.vector.tensor_scalar(out=q, in0=raw, scalar1=thr[:, 0:1], scalar2=None, op0=ALU.is_gt)
            nc.vector.tensor_scalar(out=below[:], in0=raw, scalar1=thr[:, 1:2], scalar2=None, op0=ALU.is_lt)
            nc.vector.tensor_tensor(out=q, in0=q, in1=below[:], op=ALU.subtract)
            nc.vector.quantize_mx(out=qc[:, g, :].bitcast(FP8X4), scales=qs[:, g, :], in_=q)

        codes = {}
        outs = {}
        accs = {}

        def chunk_rows(c):
            s, h = divmod(c, 4)
            return xs[s][:, 4 * h:4 * h + 4, :]

        def copy_bank(c, j, bank):
            words = chunk_rows(c)[:, j, :].bitcast(F32)
            nc.scalar.copy(
                out=words.rearrange("p (g r u) -> p g r u", g=2, u=2),
                in_=bank[:].rearrange("p (g u) r -> p g r u", u=2),
            )

        def transpose_chunk(c):
            last = None
            for j in range(4):
                bank = ps_t.tile([P, 4, P], F32, tag="tp", name="xt%d_%d" % (c, j))
                xv = chunk_rows(c)[:, j, :].bitcast(F32)
                for b in range(4):
                    nc.tensor.transpose(bank[:, b, :], xv[:, P * b:P * (b + 1)], ident[:])
                if j < 3:
                    copy_bank(c, j, bank)
                else:
                    last = bank
            return last

        def quantise_chunk(c):
            cw = cod.tile([P, K], U32, tag="codes", name="cw%d" % c, align_bytes=64)
            cs = cod.tile([P, K], U8, tag="scl", name="cs%d" % c, align_bytes=64)
            codes[c] = (cw, cs)
            nc.vector.quantize_mx(
                out=cw[:].bitcast(FP8X4), scales=cs[:],
                in_=chunk_rows(c).rearrange("p j k -> p (j k)"),
            )

        def mx_pass(c, j, g):
            cw, cs = codes[c]
            if g == 0:
                accs[(c, j)] = ps_m.tile([P, N], F32, tag="acc", name="acc%d_%d" % (c, j))
            col = (2 * j + g) * P
            nc.tensor.matmul_mx(
                out=accs[(c, j)][:],
                lhsT=cw[:, col:col + P].bitcast(FP8X4),
                lhsT_scale=cs[:, col:col + P],
                rhs=qc[:, g, :].bitcast(FP8X4),
                rhs_scale=qs[:, g, :],
                start=(g == 0),
                stop=(g == 1),
            )

        def finish_tile(c, j):
            s, h = divmod(c, 4)
            dst = outs[s][:, 4 * h + j, :]
            if j == 0 and c < CHUNKS - LAG:
                nc.scalar.copy(out=dst, in_=accs[(c, j)][:])
                nc.gpsimd.tensor_tensor(out=dst, in0=dst, in1=bias_sb[:], op=ALU.add)
            else:
                nc.vector.tensor_tensor(out=dst, in0=accs[(c, j)][:], in1=bias_sb[:], op=ALU.add)

        def store_after(c, j):
            s, h = divmod(c, 4)
            ov = out[2048 * s:2048 * (s + 1), :].rearrange("(p j) n -> p j n", j=16)
            if c >= CHUNKS - LAG:
                first, last = 4 * h + j - 1, 4 * h + j + 1
                due = j % 2 == 1
            else:
                span = STORES[s][h]
                first, last = 4 * (h + 1 - span), 4 * (h + 1)
                due = j == 3 and span > 0
            if due:
                nc.sync.dma_start(out=ov[:, first:last, :], in_=outs[s][:, first:last, :])

        def multiply_chunk(c, last_bank, first_pass_done):
            s, h = divmod(c, 4)
            if h == 0:
                outs[s] = ring.tile([P, 16, N], F32, tag="big", name="o%d" % s, align_bytes=64)
            for j in range(4):
                if not first_pass_done:
                    mx_pass(c, j, 0)
                mx_pass(c, j, 1)
                finish_tile(c, j)
                if j == 0 and last_bank is not None:
                    copy_bank(c + LAG, 3, last_bank)
                store_after(c, j)

        for r in range(CHUNKS + LAG):
            last = None
            if r < CHUNKS:
                last = transpose_chunk(r)
            if r < LAG and last is not None:
                copy_bank(r, 3, last)
                last = None
            if r == 0:
                ternarise(0)
            if 1 <= r < CHUNKS + 1:
                quantise_chunk(r - 1)
            if r == 1:
                ternarise(1)
            if r == 2:
                for j in range(4):
                    mx_pass(0, j, 0)
            if r >= LAG:
                multiply_chunk(r - LAG, last, r == LAG)
